import numpy as np
import ml_dtypes


def mxq(x, axis, fmt="e4m3"):
    dtype, down = {"e4m3": (ml_dtypes.float8_e4m3fn, 7), "e5m2": (ml_dtypes.float8_e5m2, 14)}[fmt]
    v = np.moveaxis(np.asarray(x, np.float32).astype(ml_dtypes.bfloat16).astype(np.float64), axis, -1)
    blocks = v.reshape(v.shape[:-1] + (-1, 32))
    amax = np.abs(blocks).max(-1, keepdims=True)
    byte = np.maximum(np.where(amax > 0, np.frexp(amax)[1] - 1 + 127, 0) - down, 1)
    scale = np.exp2(byte - 127.0)
    codes = (blocks / scale).astype(np.float32).astype(dtype).astype(np.float64)
    return np.moveaxis((codes * scale).reshape(v.shape), -1, axis)


WIDE = False


def mx_kscale(k):
    if not WIDE:
        return np.ones(k)
    levels = np.array([10, -10, 5, -5, 0])
    a = np.random.permutation(np.resize(levels, k // 512 * 4)).reshape(k // 512, 4)
    idx = np.arange(k)
    return np.exp2(a[idx // 512, idx % 128 // 32])


BF16 = ml_dtypes.bfloat16


def bf(x):
    return np.asarray(x, np.float32).astype(BF16)


def f64(x):
    return np.asarray(x).astype(np.float64)


B, L, D, F, K = 256, 8, 512, 1024, 16
EPS = 1e-12


def silu(v):
    return v / (1.0 + np.exp(-v))


def l2norm(t, axis):
    n = np.sqrt((t * t).sum(axis=axis, keepdims=True))
    return t / np.maximum(n, EPS)


def mix_draw(rows, cols):
    return np.random.standard_normal((L, rows, cols)) * np.sqrt(np.e / K) * np.exp(0.5 * np.random.standard_normal((L, 1, cols)))


def gain_draw():
    return (1.0 + 0.1 * np.random.standard_normal((1, F))) * np.where(np.random.standard_normal((1, F)) < 0.0, -1.0, 1.0)


def setup_inputs():
    s = mx_kscale(D)
    g = np.sqrt(np.mean(1.0 / s**2))
    return {"x": bf(np.random.standard_normal((B, L, D)) * 3.0 / np.sqrt(D) * s * g),
            "w_gate_mix": bf(mix_draw(D, F) / s[:, None]),
            "w_up_mix": bf(mix_draw(D, F) / s[:, None]),
            "u_scale_param": bf(gain_draw()),
            "v_scale_param": bf(gain_draw())}


def reference(x, w_gate_mix, w_up_mix, u_scale_param, v_scale_param):
    wg = l2norm(f64(w_gate_mix), 1)
    wu = l2norm(f64(w_up_mix), 1)
    xq = mxq(f64(x).transpose(1, 0, 2), 2, "e4m3")
    u = xq @ mxq(wg, 1, "e4m3")
    v = xq @ mxq(wu, 1, "e4m3")
    u_scale = np.abs(f64(u_scale_param))
    v_scale = np.abs(f64(v_scale_param)) * np.sqrt(D)
    h = silu(v_scale * v) * (u_scale * u)
    return h.transpose(1, 0, 2)

@@ -1,0 +1,281 @@
+import math
+from contextlib import ExitStack
+
+import concourse.mybir as mybir
+from concourse.masks import make_identity
+
+F32 = mybir.dt.float32
+BF16 = mybir.dt.bfloat16
+U32 = mybir.dt.uint32
+U8 = mybir.dt.uint8
+FP8X4 = mybir.dt.float8_e4m3fn_x4
+ACT = mybir.ActivationFunctionType
+ALU = mybir.AluOpType
+
+B, L, D, F = 256, 8, 512, 1024
+EPS = 1e-12
+FLOPS = 2 * 2 * B * L * D * F
+
+P = 128
+PACK = 4
+HALVES = B // P
+UNITS = 2
+GATE, UP = 0, 1
+BLOCKS = 2
+F_SLOT = BLOCKS * P
+SLOTS_PER_TOKEN = F // F_SLOT
+SLOTS = L * SLOTS_PER_TOKEN
+F_BLOCKS = F // P
+PREFETCH = 2
+
+
+def tile_npertokenswishglu_basis_pa_kernel(
+    tc, x, w_gate_mix, w_up_mix, u_scale_param, v_scale_param, out
+):
+    nc = tc.nc
+    with ExitStack() as ctx:
+        const = ctx.enter_context(tc.tile_pool(name="const", bufs=1))
+        weights = ctx.enter_context(tc.tile_pool(name="weights", bufs=PREFETCH + 2))
+        work = ctx.enter_context(tc.tile_pool(name="work", bufs=2))
+        small = ctx.enter_context(tc.tile_pool(name="small", bufs=3))
+        psum = ctx.enter_context(tc.psum_pool(name="psum", bufs=1))
+        ctx.enter_context(tc.manual_schedule())
+
+        gain_rows = const.tile([P, P], BF16, name="gain_rows")
+        nc.vector.memset(gain_rows[:], 0.0)
+        for unit, gain_dram in enumerate((u_scale_param, v_scale_param)):
+            nc.sync.dma_start(
+                out=gain_rows[unit * F_BLOCKS : (unit + 1) * F_BLOCKS, :],
+                in_=gain_dram.rearrange("o (r c) -> (o r) c", c=P),
+            )
+        x_sb = const.tile([P, HALVES, L, D], BF16, name="x_sb")
+        for half in range(HALVES):
+            nc.sync.dma_start(out=x_sb[:, half, :, :], in_=x[half * P : (half + 1) * P, :, :])
+
+        token_weights = {}
+
+        def load_token(token):
+            w_sb = weights.tile([P, UNITS, PACK, F], BF16, name="w_sb", tag="w_sb")
+            for unit, w_dram in enumerate((w_gate_mix, w_up_mix)):
+                nc.sync.dma_start(
+                    out=w_sb[:, unit, :, :],
+                    in_=w_dram[token].rearrange("(p j) f -> p j f", j=PACK),
+                )
+            token_weights[token] = w_sb
+
+        for token in range(PREFETCH):
+            load_token(token)
+
+        zero = const.tile([P, 1], F32, name="zero")
+        nc.vector.memset(zero[:], 0.0)
+        table_warm = const.tile([P, 1], F32, name="table_warm")
+        nc.scalar.activation(out=table_warm[:], in_=zero[:], func=ACT.Silu)
+
+        ident_bf = const.tile([P, P], BF16, name="ident_bf")
+        make_identity(nc, ident_bf[:])
+        ident_f32 = const.tile([P, P], F32, name="ident_f32")
+        make_identity(nc, ident_f32[:])
+        minus_half = const.tile([P, UNITS * BLOCKS], F32, name="minus_half")
+        nc.gpsimd.memset(minus_half[:], -0.5)
+
+        gain_T = psum.tile([P, P], BF16, name="gain_T", tag="result_T")
+        nc.tensor.transpose(gain_T[:], gain_rows[:], ident_bf[:])
+        gains = const.tile([P, UNITS * F_BLOCKS], F32, name="gains")
+        nc.scalar.activation(out=gains[:, :F_BLOCKS], in_=gain_T[:, :F_BLOCKS], func=ACT.Abs)
+        nc.scalar.activation(
+            out=gains[:, F_BLOCKS:],
+            in_=gain_T[:, F_BLOCKS : UNITS * F_BLOCKS],
+            func=ACT.Abs,
+            scale=math.sqrt(D),
+        )
+
+        x_words = x_sb[:].bitcast(F32)
+        x_grouped = const.tile([P, L, B * PACK], BF16, name="x_grouped", align_bytes=64)
+        x_codes = const.tile([P, L * B], U32, name="x_codes", align_bytes=64)
+        x_scales = const.tile([P, L * B], U8, name="x_scales", align_bytes=64)
+        for token in range(L):
+            x_T = psum.tile([P, 2, B], F32, name="x_T", tag="w_T", bufs=3)
+            for half in range(HALVES):
+                words = x_words[:, half, token, :].rearrange("p (q h) -> p h q", h=2)
+                for h in range(2):
+                    nc.tensor.transpose(
+                        x_T[:, h, half * P : (half + 1) * P], words[:, h, :], ident_f32[:]
+                    )
+            copy = nc.vector.tensor_copy if token % 2 == 0 else nc.scalar.copy
+            copy(
+                out=x_grouped[:, token, :].bitcast(F32).rearrange("p (b h) -> p b h", h=2),
+                in_=x_T[:].rearrange("p h b -> p b h"),
+            )
+        for token in range(L):
+            cols = slice(token * B, (token + 1) * B)
+            nc.vector.quantize_mx(
+                out=x_codes[:, cols].bitcast(FP8X4),
+                scales=x_scales[:, cols],
+                in_=x_grouped[:, token, :],
+            )
+
+        weights_T, square_sums, inverse_norms, spread_norms = {}, {}, {}, {}
+        normalised, codes, scales = {}, {}, {}
+        products, silu_v, results, results_T = {}, {}, {}, {}
+
+        def place(slot):
+            return slot // SLOTS_PER_TOKEN, (slot % SLOTS_PER_TOKEN) * F_SLOT
+
+        def transpose_weights(slot, unit):
+            token, f0 = place(slot)
+            w_T = psum.tile([P, BLOCKS, D], BF16, name="w_T", tag="w_T", bufs=3)
+            for block in range(BLOCKS):
+                f_cols = slice(f0 + block * P, f0 + (block + 1) * P)
+                for j in range(PACK):
+                    nc.tensor.transpose(
+                        w_T[:, block, j * P : (j + 1) * P],
+                        token_weights[token][:, unit, j, f_cols],
+                        ident_bf[:],
+                    )
+            weights_T[slot, unit] = w_T
+
+        def sum_squares(slot, unit):
+            if unit == GATE:
+                square_sums[slot] = small.tile(
+                    [P, UNITS * BLOCKS], F32, name="square_sum", tag="square_sum"
+                )
+            for block in range(BLOCKS):
+                column = unit * BLOCKS + block
+                squares = work.tile([P, D], BF16, name="squares", tag="squares", bufs=4)
+                nc.scalar.activation(
+                    out=squares[:],
+                    in_=weights_T[slot, unit][:, block, :],
+                    func=ACT.Square,
+                    accum_out=square_sums[slot][:, column : column + 1],
+                )
+
+        def invert_norms(slot):
+            clamped = small.tile([P, UNITS * BLOCKS], F32, name="clamped", tag="clamped")
+            nc.gpsimd.tensor_scalar(
+                out=clamped[:], in0=square_sums[slot][:], scalar1=EPS * EPS, scalar2=None, op0=ALU.max
+            )
+            inverse = small.tile([P, UNITS * BLOCKS], F32, name="inverse", tag="inverse")
+            nc.gpsimd.tensor_tensor(out=inverse[:], in0=clamped[:], in1=minus_half[:], op=ALU.pow)
+            inverse_norms[slot] = inverse
+
+        def spread_inverse_norms(slot):
+            spread = psum.tile([P, UNITS * F_SLOT], F32, name="spread", tag="spread", bufs=2)
+            for column in range(UNITS * BLOCKS):
+                nc.tensor.transpose(
+                    spread[:, column * P : (column + 1) * P],
+                    inverse_norms[slot][:, column : column + 1].to_broadcast([P, P]),
+                    ident_f32[:],
+                )
+            spread_norms[slot] = spread
+
+        def normalise(slot):
+            token, f0 = place(slot)
+            grouped = work.tile(
+                [P, UNITS * F_SLOT * PACK], BF16, name="grouped", tag="grouped", align_bytes=64
+            )
+            nc.vector.tensor_tensor(
+                out=grouped[:].rearrange("p (u f j) -> p u f j", u=UNITS, j=PACK),
+                in0=token_weights[token][:, :, :, f0 : f0 + F_SLOT].rearrange("p u j f -> p u f j"),
+                in1=spread_norms[slot][:]
+                .rearrange("p (u f) -> p u f", u=UNITS)
+                .unsqueeze(3)
+                .to_broadcast([P, UNITS, F_SLOT, PACK]),
+                op=ALU.mult,
+            )
+            normalised[slot] = grouped
+
+        def quantise(slot):
+            codes[slot] = work.tile(
+                [P, UNITS * F_SLOT], U32, name="w_codes", tag="w_codes", align_bytes=64
+            )
+            scales[slot] = work.tile(
+                [P, UNITS * F_SLOT], U8, name="w_scales", tag="w_scales", align_bytes=64
+            )
+            nc.vector.quantize_mx(
+                out=codes[slot][:].bitcast(FP8X4), scales=scales[slot][:], in_=normalised[slot][:]
+            )
+
+        def multiply(slot):
+            token = place(slot)[0]
+            x_cols = slice(token * B, (token + 1) * B)
+            for unit in range(UNITS):
+                product = psum.tile([P, BLOCKS, B], F32, name="product", tag="product%d" % unit)
+                for block in range(BLOCKS):
+                    w_cols = slice((unit * BLOCKS + block) * P, (unit * BLOCKS + block + 1) * P)
+                    nc.tensor.matmul_mx(
+                        out=product[:, block, :],
+                        lhsT=codes[slot][:, w_cols].bitcast(FP8X4),
+                        lhsT_scale=scales[slot][:, w_cols],
+                        rhs=x_codes[:, x_cols].bitcast(FP8X4),
+                        rhs_scale=x_scales[:, x_cols],
+                        start=True,
+                        stop=True,
+                    )
+                products[slot, unit] = product
+
+        def gain_column(slot, unit, block):
+            column = unit * F_BLOCKS + (slot % SLOTS_PER_TOKEN) * BLOCKS + block
+            return gains[:, column : column + 1]
+
+        def apply_silu(slot):
+            silu_v[slot] = work.tile([P, BLOCKS, B], F32, name="silu_v", tag="silu_v")
+            for block in range(BLOCKS):
+                nc.scalar.activation(
+                    out=silu_v[slot][:, block, :],
+                    in_=products[slot, UP][:, block, :],
+                    func=ACT.Silu,
+                    scale=gain_column(slot, UP, block),
+                )
+
+        def combine(slot):
+            results[slot] = work.tile([P, BLOCKS, B], F32, name="result", tag="result")
+            for block in range(BLOCKS):
+                nc.vector.scalar_tensor_tensor(
+                    out=results[slot][:, block, :],
+                    in0=products[slot, GATE][:, block, :],
+                    scalar=gain_column(slot, GATE, block),
+                    in1=silu_v[slot][:, block, :],
+                    op0=ALU.mult,
+                    op1=ALU.mult,
+                )
+
+        def transpose_result(slot):
+            result_T = psum.tile([P, HALVES, F_SLOT], F32, name="result_T", tag="result_T")
+            for half in range(HALVES):
+                for block in range(BLOCKS):
+                    nc.tensor.transpose(
+                        result_T[:, half, block * P : (block + 1) * P],
+                        results[slot][:, block, half * P : (half + 1) * P],
+                        ident_f32[:],
+                    )
+            results_T[slot] = result_T
+
+        def store_result(slot):
+            token, f0 = place(slot)
+            out_sb = work.tile([P, HALVES, F_SLOT], F32, name="out_sb", tag="out_sb", bufs=3)
+            nc.scalar.copy(out=out_sb[:], in_=results_T[slot][:])
+            nc.sync.dma_start(
+                out=out[:, token, f0 : f0 + F_SLOT].rearrange("(h p) f -> p h f", p=P),
+                in_=out_sb[:],
+            )
+
+        def run(stage, slot, *args):
+            if 0 <= slot < SLOTS:
+                stage(slot, *args)
+
+        for t in range(-1, SLOTS + 4):
+            if (t + 1) % SLOTS_PER_TOKEN == 0 and (t + 1) // SLOTS_PER_TOKEN + PREFETCH < L:
+                load_token((t + 1) // SLOTS_PER_TOKEN + PREFETCH)
+            run(multiply, t - 3)
+            run(transpose_result, t - 4)
+            run(spread_inverse_norms, t - 1)
+            run(transpose_weights, t + 1, GATE)
+            run(sum_squares, t, GATE)
+            run(transpose_weights, t + 1, UP)
+            run(normalise, t - 2)
+            run(apply_silu, t - 3)
+            run(sum_squares, t, UP)
+            run(invert_norms, t)
+            run(combine, t - 3)
+            run(quantise, t - 2)
+            run(store_result, t - 4)

@@ -123,15 +123,14 @@ def tile_npertokenswishglu_basis_pa_kernel(
 
         def transpose_weights(slot, unit):
             token, f0 = place(slot)
-            w_T = psum.tile([P, BLOCKS, D], BF16, name="w_T", tag="w_T", bufs=3)
-            for block in range(BLOCKS):
-                f_cols = slice(f0 + block * P, f0 + (block + 1) * P)
-                for j in range(PACK):
-                    nc.tensor.transpose(
-                        w_T[:, block, j * P : (j + 1) * P],
-                        token_weights[token][:, unit, j, f_cols],
-                        ident_bf[:],
-                    )
+            w_T = psum.tile([P, PACK * P], F32, name="w_T", tag="w_T", bufs=3)
+            words = token_weights[token][:].bitcast(F32)
+            for j in range(PACK):
+                nc.tensor.transpose(
+                    w_T[:, j * P : (j + 1) * P],
+                    words[:, unit, j, f0 // 2 : f0 // 2 + P],
+                    ident_f32[:],
+                )
             weights_T[slot, unit] = w_T
 
         def sum_squares(slot, unit):
@@ -144,7 +143,9 @@ def tile_npertokenswishglu_basis_pa_kernel(
                 squares = work.tile([P, D], BF16, name="squares", tag="squares", bufs=4)
                 nc.scalar.activation(
                     out=squares[:],
-                    in_=weights_T[slot, unit][:, block, :],
+                    in_=weights_T[slot, unit][:].bitcast(BF16).rearrange("p (w e) -> p e w", e=2)[
+                        :, block, :
+                    ],
                     func=ACT.Square,
                     accum_out=square_sums[slot][:, column : column + 1],
                 )
@@ -173,15 +174,20 @@ def tile_npertokenswishglu_basis_pa_kernel(
             grouped = work.tile(
                 [P, UNITS * F_SLOT * PACK], BF16, name="grouped", tag="grouped", align_bytes=64
             )
-            nc.vector.tensor_tensor(
-                out=grouped[:].rearrange("p (u f j) -> p u f j", u=UNITS, j=PACK),
-                in0=token_weights[token][:, :, :, f0 : f0 + F_SLOT].rearrange("p u j f -> p u f j"),
-                in1=spread_norms[slot][:]
-                .rearrange("p (u f) -> p u f", u=UNITS)
-                .unsqueeze(3)
-                .to_broadcast([P, UNITS, F_SLOT, PACK]),
-                op=ALU.mult,
-            )
+            for unit in range(UNITS):
+                nc.vector.tensor_tensor(
+                    out=grouped[:, unit * F_SLOT * PACK : (unit + 1) * F_SLOT * PACK].rearrange(
+                        "p (q e j) -> p q e j", e=2, j=PACK
+                    ),
+                    in0=token_weights[token][:, unit, :, f0 : f0 + F_SLOT].rearrange(
+                        "p j (q e) -> p q e j", e=2
+                    ),
+                    in1=spread_norms[slot][:, unit * F_SLOT : (unit + 1) * F_SLOT]
+                    .rearrange("p (e q) -> p q e", e=2)
+                    .unsqueeze(3)
+                    .to_broadcast([P, P, 2, PACK]),
+                    op=ALU.mult,
+                )
             normalised[slot] = grouped
 
         def quantise(slot):

@@ -26,7 +26,7 @@ F_SLOT = BLOCKS * P
 SLOTS_PER_TOKEN = F // F_SLOT
 SLOTS = L * SLOTS_PER_TOKEN
 F_BLOCKS = F // P
-PREFETCH = 2
+W_AHEAD = 8
 
 
 def tile_npertokenswishglu_basis_pa_kernel(
@@ -35,102 +35,117 @@ def tile_npertokenswishglu_basis_pa_kernel(
     nc = tc.nc
     with ExitStack() as ctx:
         const = ctx.enter_context(tc.tile_pool(name="const", bufs=1))
-        weights = ctx.enter_context(tc.tile_pool(name="weights", bufs=PREFETCH + 2))
+        weights = ctx.enter_context(tc.tile_pool(name="weights", bufs=W_AHEAD + 4))
         work = ctx.enter_context(tc.tile_pool(name="work", bufs=2))
         small = ctx.enter_context(tc.tile_pool(name="small", bufs=3))
         psum = ctx.enter_context(tc.psum_pool(name="psum", bufs=1))
         ctx.enter_context(tc.manual_schedule())
 
+        def place(slot):
+            return slot // SLOTS_PER_TOKEN, (slot % SLOTS_PER_TOKEN) * F_SLOT
+
+        slot_weights, x_rows = {}, {}
+
+        def load_weights(slot):
+            token, f0 = place(slot)
+            w_sb = weights.tile([P, UNITS, PACK, F_SLOT], BF16, name="w_sb", tag="w_sb")
+            for unit, w_dram in enumerate((w_gate_mix, w_up_mix)):
+                nc.sync.dma_start(
+                    out=w_sb[:, unit, :, :],
+                    in_=w_dram[token, :, f0 : f0 + F_SLOT].rearrange("(p j) f -> p j f", j=PACK),
+                )
+            slot_weights[slot] = w_sb
+
+        def load_x(token):
+            x_sb = work.tile([P, HALVES, D], BF16, name="x_sb", tag="x_sb", bufs=3)
+            nc.sync.dma_start(out=x_sb[:], in_=x[:, token, :].rearrange("(h p) d -> p h d", p=P))
+            x_rows[token] = x_sb
+
         gain_rows = const.tile([P, P], BF16, name="gain_rows")
         nc.vector.memset(gain_rows[:], 0.0)
+
+        load_weights(0)
+        load_x(0)
         for unit, gain_dram in enumerate((u_scale_param, v_scale_param)):
             nc.sync.dma_start(
                 out=gain_rows[unit * F_BLOCKS : (unit + 1) * F_BLOCKS, :],
                 in_=gain_dram.rearrange("o (r c) -> (o r) c", c=P),
             )
-        x_sb = const.tile([P, HALVES, L, D], BF16, name="x_sb")
-        for half in range(HALVES):
-            nc.sync.dma_start(out=x_sb[:, half, :, :], in_=x[half * P : (half + 1) * P, :, :])
-
-        token_weights = {}
-
-        def load_token(token):
-            w_sb = weights.tile([P, UNITS, PACK, F], BF16, name="w_sb", tag="w_sb")
-            for unit, w_dram in enumerate((w_gate_mix, w_up_mix)):
-                nc.sync.dma_start(
-                    out=w_sb[:, unit, :, :],
-                    in_=w_dram[token].rearrange("(p j) f -> p j f", j=PACK),
-                )
-            token_weights[token] = w_sb
-
-        for token in range(PREFETCH):
-            load_token(token)
+        for slot in range(1, W_AHEAD):
+            load_weights(slot)
+            if slot == SLOTS_PER_TOKEN:
+                load_x(1)
 
         zero = const.tile([P, 1], F32, name="zero")
         nc.vector.memset(zero[:], 0.0)
         table_warm = const.tile([P, 1], F32, name="table_warm")
         nc.scalar.activation(out=table_warm[:], in_=zero[:], func=ACT.Silu)
 
-        ident_bf = const.tile([P, P], BF16, name="ident_bf")
-        make_identity(nc, ident_bf[:])
         ident_f32 = const.tile([P, P], F32, name="ident_f32")
         make_identity(nc, ident_f32[:])
+        ident_bf = const.tile([P, P], BF16, name="ident_bf")
+        make_identity(nc, ident_bf[:])
         minus_half = const.tile([P, UNITS * BLOCKS], F32, name="minus_half")
         nc.gpsimd.memset(minus_half[:], -0.5)
+        gains = const.tile([P, UNITS * F_BLOCKS], F32, name="gains")
 
         gain_T = psum.tile([P, P], BF16, name="gain_T", tag="result_T")
-        nc.tensor.transpose(gain_T[:], gain_rows[:], ident_bf[:])
-        gains = const.tile([P, UNITS * F_BLOCKS], F32, name="gains")
-        nc.scalar.activation(out=gains[:, :F_BLOCKS], in_=gain_T[:, :F_BLOCKS], func=ACT.Abs)
-        nc.scalar.activation(
-            out=gains[:, F_BLOCKS:],
-            in_=gain_T[:, F_BLOCKS : UNITS * F_BLOCKS],
-            func=ACT.Abs,
-            scale=math.sqrt(D),
-        )
 
-        x_words = x_sb[:].bitcast(F32)
-        x_grouped = const.tile([P, L, B * PACK], BF16, name="x_grouped", align_bytes=64)
-        x_codes = const.tile([P, L * B], U32, name="x_codes", align_bytes=64)
-        x_scales = const.tile([P, L * B], U8, name="x_scales", align_bytes=64)
-        for token in range(L):
-            x_T = psum.tile([P, 2, B], F32, name="x_T", tag="w_T", bufs=3)
+        def transpose_gains():
+            nc.tensor.transpose(gain_T[:], gain_rows[:], ident_bf[:])
+
+        def scale_gains():
+            nc.scalar.activation(out=gains[:, :F_BLOCKS], in_=gain_T[:, :F_BLOCKS], func=ACT.Abs)
+            nc.scalar.activation(
+                out=gains[:, F_BLOCKS:],
+                in_=gain_T[:, F_BLOCKS : UNITS * F_BLOCKS],
+                func=ACT.Abs,
+                scale=math.sqrt(D),
+            )
+
+        x_turned, x_grouped, x_codes, x_scales = {}, {}, {}, {}
+
+        def transpose_x(token):
+            if token == 0:
+                x_T = psum.tile([P, 2, B], F32, name="x_T", tag="product0")
+            else:
+                x_T = psum.tile([P, 2, B], F32, name="x_T", tag="w_T", bufs=3)
+            x_words = x_rows[token][:].bitcast(F32)
             for half in range(HALVES):
-                words = x_words[:, half, token, :].rearrange("p (q h) -> p h q", h=2)
+                words = x_words[:, half, :].rearrange("p (q h) -> p h q", h=2)
                 for h in range(2):
                     nc.tensor.transpose(
                         x_T[:, h, half * P : (half + 1) * P], words[:, h, :], ident_f32[:]
                     )
+            x_turned[token] = x_T
+
+        def group_x(token):
+            grouped = work.tile([P, B * PACK], BF16, name="x_grouped", tag="x_grouped", align_bytes=64)
             copy = nc.vector.tensor_copy if token % 2 == 0 else nc.scalar.copy
             copy(
-                out=x_grouped[:, token, :].bitcast(F32).rearrange("p (b h) -> p b h", h=2),
-                in_=x_T[:].rearrange("p h b -> p b h"),
+                out=grouped[:].bitcast(F32).rearrange("p (b h) -> p b h", h=2),
+                in_=x_turned[token][:].rearrange("p h b -> p b h"),
             )
-        for token in range(L):
-            cols = slice(token * B, (token + 1) * B)
+            x_grouped[token] = grouped
+
+        def quantise_x(token):
+            x_codes[token] = const.tile([P, B], U32, name="x_codes%d" % token, align_bytes=64)
+            x_scales[token] = const.tile([P, B], U8, name="x_scales%d" % token, align_bytes=64)
             nc.vector.quantize_mx(
-                out=x_codes[:, cols].bitcast(FP8X4),
-                scales=x_scales[:, cols],
-                in_=x_grouped[:, token, :],
+                out=x_codes[token][:].bitcast(FP8X4),
+                scales=x_scales[token][:],
+                in_=x_grouped[token][:],
             )
 
         weights_T, square_sums, inverse_norms, spread_norms = {}, {}, {}, {}
         normalised, codes, scales = {}, {}, {}
         products, silu_v, results, results_T = {}, {}, {}, {}
 
-        def place(slot):
-            return slot // SLOTS_PER_TOKEN, (slot % SLOTS_PER_TOKEN) * F_SLOT
-
         def transpose_weights(slot, unit):
-            token, f0 = place(slot)
             w_T = psum.tile([P, PACK * P], F32, name="w_T", tag="w_T", bufs=3)
-            words = token_weights[token][:].bitcast(F32)
+            words = slot_weights[slot][:].bitcast(F32)
             for j in range(PACK):
-                nc.tensor.transpose(
-                    w_T[:, j * P : (j + 1) * P],
-                    words[:, unit, j, f0 // 2 : f0 // 2 + P],
-                    ident_f32[:],
-                )
+                nc.tensor.transpose(w_T[:, j * P : (j + 1) * P], words[:, unit, j, :], ident_f32[:])
             weights_T[slot, unit] = w_T
 
         def sum_squares(slot, unit):
@@ -138,14 +153,13 @@ def tile_npertokenswishglu_basis_pa_kernel(
                 square_sums[slot] = small.tile(
                     [P, UNITS * BLOCKS], F32, name="square_sum", tag="square_sum"
                 )
-            for block in range(BLOCKS):
-                column = unit * BLOCKS + block
+            halves_of_words = weights_T[slot, unit][:].bitcast(BF16).rearrange("p (w e) -> p e w", e=2)
+            for e in range(2):
+                column = unit * BLOCKS + e
                 squares = work.tile([P, D], BF16, name="squares", tag="squares", bufs=4)
                 nc.scalar.activation(
                     out=squares[:],
-                    in_=weights_T[slot, unit][:].bitcast(BF16).rearrange("p (w e) -> p e w", e=2)[
-                        :, block, :
-                    ],
+                    in_=halves_of_words[:, e, :],
                     func=ACT.Square,
                     accum_out=square_sums[slot][:, column : column + 1],
                 )
@@ -170,7 +184,6 @@ def tile_npertokenswishglu_basis_pa_kernel(
             spread_norms[slot] = spread
 
         def normalise(slot):
-            token, f0 = place(slot)
             grouped = work.tile(
                 [P, UNITS * F_SLOT * PACK], BF16, name="grouped", tag="grouped", align_bytes=64
             )
@@ -179,9 +192,7 @@ def tile_npertokenswishglu_basis_pa_kernel(
                     out=grouped[:, unit * F_SLOT * PACK : (unit + 1) * F_SLOT * PACK].rearrange(
                         "p (q e j) -> p q e j", e=2, j=PACK
                     ),
-                    in0=token_weights[token][:, unit, :, f0 : f0 + F_SLOT].rearrange(
-                        "p j (q e) -> p q e j", e=2
-                    ),
+                    in0=slot_weights[slot][:, unit, :, :].rearrange("p j (q e) -> p q e j", e=2),
                     in1=spread_norms[slot][:, unit * F_SLOT : (unit + 1) * F_SLOT]
                     .rearrange("p (e q) -> p q e", e=2)
                     .unsqueeze(3)
@@ -203,7 +214,6 @@ def tile_npertokenswishglu_basis_pa_kernel(
 
         def multiply(slot):
             token = place(slot)[0]
-            x_cols = slice(token * B, (token + 1) * B)
             for unit in range(UNITS):
                 product = psum.tile([P, BLOCKS, B], F32, name="product", tag="product%d" % unit)
                 for block in range(BLOCKS):
@@ -212,8 +222,8 @@ def tile_npertokenswishglu_basis_pa_kernel(
                         out=product[:, block, :],
                         lhsT=codes[slot][:, w_cols].bitcast(FP8X4),
                         lhsT_scale=scales[slot][:, w_cols],
-                        rhs=x_codes[:, x_cols].bitcast(FP8X4),
-                        rhs_scale=x_scales[:, x_cols],
+                        rhs=x_codes[token][:].bitcast(FP8X4),
+                        rhs_scale=x_scales[token][:],
                         start=True,
                         stop=True,
                     )
@@ -269,9 +279,17 @@ def tile_npertokenswishglu_basis_pa_kernel(
             if 0 <= slot < SLOTS:
                 stage(slot, *args)
 
+        X_LEAD = 2
+        turn_at, quantise_at = {-1: 0}, {0: 0}
+        for token in range(1, L):
+            turn_at[SLOTS_PER_TOKEN * token - X_LEAD] = token
+            quantise_at[SLOTS_PER_TOKEN * token - X_LEAD + 1] = token
+
         for t in range(-1, SLOTS + 4):
-            if (t + 1) % SLOTS_PER_TOKEN == 0 and (t + 1) // SLOTS_PER_TOKEN + PREFETCH < L:
-                load_token((t + 1) // SLOTS_PER_TOKEN + PREFETCH)
+            if t >= 0:
+                run(load_weights, t + W_AHEAD)
+            if turn_at.get(t, 0) > 0 and turn_at[t] + 1 < L:
+                load_x(turn_at[t] + 1)
             run(multiply, t - 3)
             run(transpose_result, t - 4)
             run(spread_inverse_norms, t - 1)
@@ -281,7 +299,17 @@ def tile_npertokenswishglu_basis_pa_kernel(
             run(normalise, t - 2)
             run(apply_silu, t - 3)
             run(sum_squares, t, UP)
+            if t in turn_at:
+                transpose_x(turn_at[t])
+            if t == -1:
+                transpose_gains()
+            if t == 1:
+                scale_gains()
             run(invert_norms, t)
             run(combine, t - 3)
             run(quantise, t - 2)
+            if t in turn_at:
+                group_x(turn_at[t])
+            if t in quantise_at:
+                quantise_x(quantise_at[t])
             run(store_result, t - 4)

@@ -137,7 +137,7 @@ def tile_npertokenswishglu_basis_pa_kernel(
                 in_=x_grouped[token][:],
             )
 
-        weights_T, square_sums, inverse_norms, spread_norms = {}, {}, {}, {}
+        weights_T, square_sums, clamped_sums, inverse_norms, spread_norms = {}, {}, {}, {}, {}
         normalised, codes, scales = {}, {}, {}
         products, silu_v, results, results_T = {}, {}, {}, {}
 
@@ -164,13 +164,18 @@ def tile_npertokenswishglu_basis_pa_kernel(
                     accum_out=square_sums[slot][:, column : column + 1],
                 )
 
-        def invert_norms(slot):
+        def clamp_sums(slot):
             clamped = small.tile([P, UNITS * BLOCKS], F32, name="clamped", tag="clamped")
-            nc.gpsimd.tensor_scalar(
+            nc.vector.tensor_scalar(
                 out=clamped[:], in0=square_sums[slot][:], scalar1=EPS * EPS, scalar2=None, op0=ALU.max
             )
+            clamped_sums[slot] = clamped
+
+        def invert_norms(slot):
             inverse = small.tile([P, UNITS * BLOCKS], F32, name="inverse", tag="inverse")
-            nc.gpsimd.tensor_tensor(out=inverse[:], in0=clamped[:], in1=minus_half[:], op=ALU.pow)
+            nc.gpsimd.tensor_tensor(
+                out=inverse[:], in0=clamped_sums[slot][:], in1=minus_half[:], op=ALU.pow
+            )
             inverse_norms[slot] = inverse
 
         def spread_inverse_norms(slot):
@@ -290,10 +295,12 @@ def tile_npertokenswishglu_basis_pa_kernel(
                 run(load_weights, t + W_AHEAD)
             if turn_at.get(t, 0) > 0 and turn_at[t] + 1 < L:
                 load_x(turn_at[t] + 1)
+            run(clamp_sums, t - 1)
+            run(invert_norms, t - 1)
             run(multiply, t - 3)
             run(transpose_result, t - 4)
-            run(spread_inverse_norms, t - 1)
             run(transpose_weights, t + 1, GATE)
+            run(spread_inverse_norms, t - 1)
             run(sum_squares, t, GATE)
             run(transpose_weights, t + 1, UP)
             run(normalise, t - 2)
@@ -305,7 +312,6 @@ def tile_npertokenswishglu_basis_pa_kernel(
                 transpose_gains()
             if t == 1:
                 scale_gains()
-            run(invert_norms, t)
             run(combine, t - 3)
             run(quantise, t - 2)
             if t in turn_at:

@@ -27,6 +27,8 @@ SLOTS_PER_TOKEN = F // F_SLOT
 SLOTS = L * SLOTS_PER_TOKEN
 F_BLOCKS = F // P
 W_AHEAD = 8
+G_WORDS = 32
+V_WORDS = P - G_WORDS
 
 
 def tile_npertokenswishglu_basis_pa_kernel(
@@ -138,7 +140,7 @@ def tile_npertokenswishglu_basis_pa_kernel(
             )
 
         weights_T, square_sums, clamped_sums, inverse_norms, spread_norms = {}, {}, {}, {}, {}
-        normalised, codes, scales = {}, {}, {}
+        inverse_rows, normalised, codes, scales = {}, {}, {}, {}
         products, silu_v, results, results_T = {}, {}, {}, {}
 
         def transpose_weights(slot, unit):
@@ -188,23 +190,51 @@ def tile_npertokenswishglu_basis_pa_kernel(
                 )
             spread_norms[slot] = spread
 
+        def copy_inverse(slot):
+            rows = small.tile([P, UNITS * BLOCKS, G_WORDS], F32, name="inverse_rows", tag="inverse_rows")
+            nc.scalar.copy(
+                out=rows[:],
+                in_=spread_norms[slot][:].rearrange("p (c q) -> p c q", q=P)[:, :, V_WORDS:],
+            )
+            inverse_rows[slot] = rows
+
         def normalise(slot):
             grouped = work.tile(
                 [P, UNITS * F_SLOT * PACK], BF16, name="grouped", tag="grouped", align_bytes=64
             )
             for unit in range(UNITS):
+                first = unit * F_SLOT * PACK
                 nc.vector.tensor_tensor(
-                    out=grouped[:, unit * F_SLOT * PACK : (unit + 1) * F_SLOT * PACK].rearrange(
+                    out=grouped[:, first : first + V_WORDS * 2 * PACK].rearrange(
                         "p (q e j) -> p q e j", e=2, j=PACK
                     ),
-                    in0=slot_weights[slot][:, unit, :, :].rearrange("p j (q e) -> p q e j", e=2),
+                    in0=slot_weights[slot][:, unit, :, : V_WORDS * 2].rearrange(
+                        "p j (q e) -> p q e j", e=2
+                    ),
                     in1=spread_norms[slot][:, unit * F_SLOT : (unit + 1) * F_SLOT]
-                    .rearrange("p (e q) -> p q e", e=2)
+                    .rearrange("p (e q) -> p q e", e=2)[:, :V_WORDS, :]
                     .unsqueeze(3)
-                    .to_broadcast([P, P, 2, PACK]),
+                    .to_broadcast([P, V_WORDS, 2, PACK]),
                     op=ALU.mult,
                 )
             normalised[slot] = grouped
+
+        def normalise_rest(slot):
+            for unit in range(UNITS):
+                first = unit * F_SLOT * PACK + V_WORDS * 2 * PACK
+                nc.gpsimd.tensor_tensor(
+                    out=normalised[slot][:, first : first + G_WORDS * 2 * PACK].rearrange(
+                        "p (q e j) -> p q e j", e=2, j=PACK
+                    ),
+                    in0=slot_weights[slot][:, unit, :, V_WORDS * 2 :].rearrange(
+                        "p j (q e) -> p q e j", e=2
+                    ),
+                    in1=inverse_rows[slot][:, unit * BLOCKS : (unit + 1) * BLOCKS, :]
+                    .rearrange("p e q -> p q e")
+                    .unsqueeze(3)
+                    .to_broadcast([P, G_WORDS, 2, PACK]),
+                    op=ALU.mult,
+                )
 
         def quantise(slot):
             codes[slot] = work.tile(
@@ -296,14 +326,16 @@ def tile_npertokenswishglu_basis_pa_kernel(
             if turn_at.get(t, 0) > 0 and turn_at[t] + 1 < L:
                 load_x(turn_at[t] + 1)
             run(clamp_sums, t - 1)
-            run(invert_norms, t - 1)
+            run(copy_inverse, t - 2)
             run(multiply, t - 3)
             run(transpose_result, t - 4)
             run(transpose_weights, t + 1, GATE)
-            run(spread_inverse_norms, t - 1)
             run(sum_squares, t, GATE)
             run(transpose_weights, t + 1, UP)
             run(normalise, t - 2)
+            run(normalise_rest, t - 2)
+            run(invert_norms, t - 1)
+            run(spread_inverse_norms, t - 1)
             run(apply_silu, t - 3)
             run(sum_squares, t, UP)
             if t in turn_at:

@@ -27,8 +27,9 @@ SLOTS_PER_TOKEN = F // F_SLOT
 SLOTS = L * SLOTS_PER_TOKEN
 F_BLOCKS = F // P
 W_AHEAD = 8
-G_WORDS = 32
-V_WORDS = P - G_WORDS
+G_FEATURES = 64
+V_FEATURES = F_SLOT - G_FEATURES
+GRAM_SLOTS = (0, 3, 6)
 
 
 def tile_npertokenswishglu_basis_pa_kernel(
@@ -37,9 +38,9 @@ def tile_npertokenswishglu_basis_pa_kernel(
     nc = tc.nc
     with ExitStack() as ctx:
         const = ctx.enter_context(tc.tile_pool(name="const", bufs=1))
-        weights = ctx.enter_context(tc.tile_pool(name="weights", bufs=W_AHEAD + 4))
+        weights = ctx.enter_context(tc.tile_pool(name="weights", bufs=W_AHEAD + 6))
         work = ctx.enter_context(tc.tile_pool(name="work", bufs=2))
-        small = ctx.enter_context(tc.tile_pool(name="small", bufs=3))
+        small = ctx.enter_context(tc.tile_pool(name="small", bufs=4))
         psum = ctx.enter_context(tc.psum_pool(name="psum", bufs=1))
         ctx.enter_context(tc.manual_schedule())
 
@@ -123,7 +124,7 @@ def tile_npertokenswishglu_basis_pa_kernel(
 
         def group_x(token):
             grouped = work.tile([P, B * PACK], BF16, name="x_grouped", tag="x_grouped", align_bytes=64)
-            copy = nc.vector.tensor_copy if token % 2 == 0 else nc.scalar.copy
+            copy = nc.vector.tensor_copy
             copy(
                 out=grouped[:].bitcast(F32).rearrange("p (b h) -> p b h", h=2),
                 in_=x_turned[token][:].rearrange("p h b -> p b h"),
@@ -139,22 +140,54 @@ def tile_npertokenswishglu_basis_pa_kernel(
                 in_=x_grouped[token][:],
             )
 
-        weights_T, square_sums, clamped_sums, inverse_norms, spread_norms = {}, {}, {}, {}, {}
+        weights_T, square_sums, inverse_norms, spread_norms = {}, {}, {}, {}
         inverse_rows, normalised, codes, scales = {}, {}, {}, {}
         products, silu_v, results, results_T = {}, {}, {}, {}
 
         def transpose_weights(slot, unit):
             w_T = psum.tile([P, PACK * P], F32, name="w_T", tag="w_T", bufs=3)
-            words = slot_weights[slot][:].bitcast(F32)
-            for j in range(PACK):
-                nc.tensor.transpose(w_T[:, j * P : (j + 1) * P], words[:, unit, j, :], ident_f32[:])
+            if uses_gram(slot, unit):
+                for block in range(BLOCKS):
+                    for j in range(PACK):
+                        w_block = slot_weights[slot][:, unit, j, block * P : (block + 1) * P]
+                        nc.tensor.matmul(
+                            out=w_T[:, block * P : (block + 1) * P],
+                            lhsT=w_block,
+                            rhs=w_block,
+                            start=(j == 0),
+                            stop=(j == PACK - 1),
+                        )
+            else:
+                words = slot_weights[slot][:].bitcast(F32)
+                for j in range(PACK):
+                    nc.tensor.transpose(
+                        w_T[:, j * P : (j + 1) * P], words[:, unit, j, :], ident_f32[:]
+                    )
             weights_T[slot, unit] = w_T
 
-        def sum_squares(slot, unit):
-            if unit == GATE:
-                square_sums[slot] = small.tile(
-                    [P, UNITS * BLOCKS], F32, name="square_sum", tag="square_sum"
+        def uses_gram(slot, unit):
+            return unit == GATE and slot % 8 in GRAM_SLOTS
+
+        def take_diagonal(slot, unit):
+            for block in range(BLOCKS):
+                column = unit * BLOCKS + block
+                masked = work.tile([P, P], F32, name="masked", tag="masked")
+                nc.vector.scalar_tensor_tensor(
+                    out=masked[:],
+                    in0=weights_T[slot, unit][:, block * P : (block + 1) * P],
+                    scalar=1.0,
+                    in1=ident_f32[:],
+                    op0=ALU.mult,
+                    op1=ALU.mult,
+                    accum_out=square_sums[slot][:, column : column + 1],
                 )
+
+        def new_sums(slot):
+            square_sums[slot] = small.tile(
+                [P, UNITS * BLOCKS], F32, name="square_sum", tag="square_sum"
+            )
+
+        def sum_squares(slot, unit):
             halves_of_words = weights_T[slot, unit][:].bitcast(BF16).rearrange("p (w e) -> p e w", e=2)
             for e in range(2):
                 column = unit * BLOCKS + e
@@ -166,35 +199,35 @@ def tile_npertokenswishglu_basis_pa_kernel(
                     accum_out=square_sums[slot][:, column : column + 1],
                 )
 
-        def clamp_sums(slot):
+        def invert_norms(slot):
             clamped = small.tile([P, UNITS * BLOCKS], F32, name="clamped", tag="clamped")
-            nc.vector.tensor_scalar(
+            nc.gpsimd.tensor_scalar(
                 out=clamped[:], in0=square_sums[slot][:], scalar1=EPS * EPS, scalar2=None, op0=ALU.max
             )
-            clamped_sums[slot] = clamped
-
-        def invert_norms(slot):
             inverse = small.tile([P, UNITS * BLOCKS], F32, name="inverse", tag="inverse")
-            nc.gpsimd.tensor_tensor(
-                out=inverse[:], in0=clamped_sums[slot][:], in1=minus_half[:], op=ALU.pow
-            )
+            nc.gpsimd.tensor_tensor(out=inverse[:], in0=clamped[:], in1=minus_half[:], op=ALU.pow)
             inverse_norms[slot] = inverse
 
         def spread_inverse_norms(slot):
             spread = psum.tile([P, UNITS * F_SLOT], F32, name="spread", tag="spread", bufs=2)
-            for column in range(UNITS * BLOCKS):
-                nc.tensor.transpose(
-                    spread[:, column * P : (column + 1) * P],
-                    inverse_norms[slot][:, column : column + 1].to_broadcast([P, P]),
-                    ident_f32[:],
-                )
+            by_column = spread[:].rearrange("p (u q e) -> p u e q", u=UNITS, e=2)
+            for unit in range(UNITS):
+                for e in range(2):
+                    column = unit * BLOCKS + e
+                    nc.tensor.transpose(
+                        spread[:, column * P : (column + 1) * P]
+                        if uses_gram(slot, unit)
+                        else by_column[:, unit, e, :],
+                        inverse_norms[slot][:, column : column + 1].to_broadcast([P, P]),
+                        ident_f32[:],
+                    )
             spread_norms[slot] = spread
 
         def copy_inverse(slot):
-            rows = small.tile([P, UNITS * BLOCKS, G_WORDS], F32, name="inverse_rows", tag="inverse_rows")
+            rows = small.tile([P, UNITS, G_FEATURES], F32, name="inverse_rows", tag="inverse_rows")
             nc.scalar.copy(
                 out=rows[:],
-                in_=spread_norms[slot][:].rearrange("p (c q) -> p c q", q=P)[:, :, V_WORDS:],
+                in_=spread_norms[slot][:].rearrange("p (u f) -> p u f", u=UNITS)[:, :, V_FEATURES:],
             )
             inverse_rows[slot] = rows
 
@@ -202,39 +235,26 @@ def tile_npertokenswishglu_basis_pa_kernel(
             grouped = work.tile(
                 [P, UNITS * F_SLOT * PACK], BF16, name="grouped", tag="grouped", align_bytes=64
             )
-            for unit in range(UNITS):
-                first = unit * F_SLOT * PACK
-                nc.vector.tensor_tensor(
-                    out=grouped[:, first : first + V_WORDS * 2 * PACK].rearrange(
-                        "p (q e j) -> p q e j", e=2, j=PACK
-                    ),
-                    in0=slot_weights[slot][:, unit, :, : V_WORDS * 2].rearrange(
-                        "p j (q e) -> p q e j", e=2
-                    ),
-                    in1=spread_norms[slot][:, unit * F_SLOT : (unit + 1) * F_SLOT]
-                    .rearrange("p (e q) -> p q e", e=2)[:, :V_WORDS, :]
-                    .unsqueeze(3)
-                    .to_broadcast([P, V_WORDS, 2, PACK]),
-                    op=ALU.mult,
-                )
+            nc.vector.tensor_tensor(
+                out=grouped[:].rearrange("p (u f j) -> p u f j", u=UNITS, j=PACK)[:, :, :V_FEATURES, :],
+                in0=slot_weights[slot][:].rearrange("p u j f -> p u f j")[:, :, :V_FEATURES, :],
+                in1=spread_norms[slot][:]
+                .rearrange("p (u f) -> p u f", u=UNITS)[:, :, :V_FEATURES]
+                .unsqueeze(3)
+                .to_broadcast([P, UNITS, V_FEATURES, PACK]),
+                op=ALU.mult,
+            )
             normalised[slot] = grouped
 
         def normalise_rest(slot):
-            for unit in range(UNITS):
-                first = unit * F_SLOT * PACK + V_WORDS * 2 * PACK
-                nc.gpsimd.tensor_tensor(
-                    out=normalised[slot][:, first : first + G_WORDS * 2 * PACK].rearrange(
-                        "p (q e j) -> p q e j", e=2, j=PACK
-                    ),
-                    in0=slot_weights[slot][:, unit, :, V_WORDS * 2 :].rearrange(
-                        "p j (q e) -> p q e j", e=2
-                    ),
-                    in1=inverse_rows[slot][:, unit * BLOCKS : (unit + 1) * BLOCKS, :]
-                    .rearrange("p e q -> p q e")
-                    .unsqueeze(3)
-                    .to_broadcast([P, G_WORDS, 2, PACK]),
-                    op=ALU.mult,
-                )
+            nc.gpsimd.tensor_tensor(
+                out=normalised[slot][:].rearrange("p (u f j) -> p u f j", u=UNITS, j=PACK)[
+                    :, :, V_FEATURES:, :
+                ],
+                in0=slot_weights[slot][:].rearrange("p u j f -> p u f j")[:, :, V_FEATURES:, :],
+                in1=inverse_rows[slot][:].unsqueeze(3).to_broadcast([P, UNITS, G_FEATURES, PACK]),
+                op=ALU.mult,
+            )
 
         def quantise(slot):
             codes[slot] = work.tile(
@@ -314,40 +334,43 @@ def tile_npertokenswishglu_basis_pa_kernel(
             if 0 <= slot < SLOTS:
                 stage(slot, *args)
 
-        X_LEAD = 2
-        turn_at, quantise_at = {-1: 0}, {0: 0}
+        X_LEAD = 5
+        turn_at, quantise_at = {-4: 0}, {-3: 0}
         for token in range(1, L):
             turn_at[SLOTS_PER_TOKEN * token - X_LEAD] = token
             quantise_at[SLOTS_PER_TOKEN * token - X_LEAD + 1] = token
 
-        for t in range(-1, SLOTS + 4):
-            if t >= 0:
-                run(load_weights, t + W_AHEAD)
+        for t in range(-4, SLOTS + 2):
+            if t >= -3:
+                run(load_weights, t + 3 + W_AHEAD)
             if turn_at.get(t, 0) > 0 and turn_at[t] + 1 < L:
                 load_x(turn_at[t] + 1)
-            run(clamp_sums, t - 1)
-            run(copy_inverse, t - 2)
-            run(multiply, t - 3)
-            run(transpose_result, t - 4)
-            run(transpose_weights, t + 1, GATE)
-            run(sum_squares, t, GATE)
-            run(transpose_weights, t + 1, UP)
-            run(normalise, t - 2)
-            run(normalise_rest, t - 2)
-            run(invert_norms, t - 1)
-            run(spread_inverse_norms, t - 1)
-            run(apply_silu, t - 3)
-            run(sum_squares, t, UP)
+            run(multiply, t - 1)
+            run(transpose_result, t - 2)
+            run(spread_inverse_norms, t + 1)
+            run(transpose_weights, t + 4, GATE)
+            run(new_sums, t + 3)
+            if uses_gram(t + 3, GATE):
+                run(take_diagonal, t + 3, GATE)
+            else:
+                run(sum_squares, t + 3, GATE)
+            run(transpose_weights, t + 4, UP)
+            run(normalise, t)
+            run(normalise_rest, t)
+            run(invert_norms, t + 2)
+            run(apply_silu, t - 1)
+            run(sum_squares, t + 3, UP)
+            run(copy_inverse, t + 1)
             if t in turn_at:
                 transpose_x(turn_at[t])
-            if t == -1:
+            if t == -4:
                 transpose_gains()
-            if t == 1:
+            if t == -2:
                 scale_gains()
-            run(combine, t - 3)
-            run(quantise, t - 2)
+            run(combine, t - 1)
+            run(quantise, t)
             if t in turn_at:
                 group_x(turn_at[t])
             if t in quantise_at:
                 quantise_x(quantise_at[t])
-            run(store_result, t - 4)
+            run(store_result, t - 2)

@@ -42,7 +42,6 @@ def tile_npertokenswishglu_basis_pa_kernel(
         work = ctx.enter_context(tc.tile_pool(name="work", bufs=2))
         small = ctx.enter_context(tc.tile_pool(name="small", bufs=4))
         psum = ctx.enter_context(tc.psum_pool(name="psum", bufs=1))
-        ctx.enter_context(tc.manual_schedule())
 
         def place(slot):
             return slot // SLOTS_PER_TOKEN, (slot % SLOTS_PER_TOKEN) * F_SLOT

@@ -27,7 +27,7 @@ SLOTS_PER_TOKEN = F // F_SLOT
 SLOTS = L * SLOTS_PER_TOKEN
 F_BLOCKS = F // P
 W_AHEAD = 8
-G_FEATURES = 64
+G_FEATURES = 56
 V_FEATURES = F_SLOT - G_FEATURES
 GRAM_SLOTS = (0, 3, 6)
 

@@ -39,8 +39,8 @@ def tile_npertokenswishglu_basis_pa_kernel(
     with ExitStack() as ctx:
         const = ctx.enter_context(tc.tile_pool(name="const", bufs=1))
         weights = ctx.enter_context(tc.tile_pool(name="weights", bufs=W_AHEAD + 6))
-        work = ctx.enter_context(tc.tile_pool(name="work", bufs=2))
-        small = ctx.enter_context(tc.tile_pool(name="small", bufs=4))
+        work = ctx.enter_context(tc.tile_pool(name="work", bufs=3))
+        small = ctx.enter_context(tc.tile_pool(name="small", bufs=6))
         psum = ctx.enter_context(tc.psum_pool(name="psum", bufs=1))
 
         def place(slot):
@@ -322,7 +322,7 @@ def tile_npertokenswishglu_basis_pa_kernel(
 
         def store_result(slot):
             token, f0 = place(slot)
-            out_sb = work.tile([P, HALVES, F_SLOT], F32, name="out_sb", tag="out_sb", bufs=3)
+            out_sb = work.tile([P, HALVES, F_SLOT], F32, name="out_sb", tag="out_sb", bufs=4)
             nc.scalar.copy(out=out_sb[:], in_=results_T[slot][:])
             nc.sync.dma_start(
                 out=out[:, token, f0 : f0 + F_SLOT].rearrange("(h p) f -> p h f", p=P),

@@ -232,7 +232,7 @@ def tile_npertokenswishglu_basis_pa_kernel(
 
         def normalise(slot):
             grouped = work.tile(
-                [P, UNITS * F_SLOT * PACK], BF16, name="grouped", tag="grouped", align_bytes=64
+                [P, UNITS * F_SLOT * PACK], BF16, name="grouped", tag="grouped", bufs=1, align_bytes=64
             )
             nc.vector.tensor_tensor(
                 out=grouped[:].rearrange("p (u f j) -> p u f j", u=UNITS, j=PACK)[:, :, :V_FEATURES, :],

@@ -27,8 +27,8 @@ SLOTS_PER_TOKEN = F // F_SLOT
 SLOTS = L * SLOTS_PER_TOKEN
 F_BLOCKS = F // P
 W_AHEAD = 8
-G_FEATURES = 56
-V_FEATURES = F_SLOT - G_FEATURES
+G_COLUMNS = 112
+V_COLUMNS = UNITS * F_SLOT - G_COLUMNS
 GRAM_SLOTS = (0, 3, 6)
 
 
@@ -50,10 +50,10 @@ def tile_npertokenswishglu_basis_pa_kernel(
 
         def load_weights(slot):
             token, f0 = place(slot)
-            w_sb = weights.tile([P, UNITS, PACK, F_SLOT], BF16, name="w_sb", tag="w_sb")
+            w_sb = weights.tile([P, PACK, UNITS, F_SLOT], BF16, name="w_sb", tag="w_sb")
             for unit, w_dram in enumerate((w_gate_mix, w_up_mix)):
                 nc.sync.dma_start(
-                    out=w_sb[:, unit, :, :],
+                    out=w_sb[:, :, unit, :],
                     in_=w_dram[token, :, f0 : f0 + F_SLOT].rearrange("(p j) f -> p j f", j=PACK),
                 )
             slot_weights[slot] = w_sb
@@ -123,7 +123,7 @@ def tile_npertokenswishglu_basis_pa_kernel(
 
         def group_x(token):
             grouped = work.tile([P, B * PACK], BF16, name="x_grouped", tag="x_grouped", align_bytes=64)
-            copy = nc.vector.tensor_copy
+            copy = nc.vector.tensor_copy if token == 0 else nc.scalar.copy
             copy(
                 out=grouped[:].bitcast(F32).rearrange("p (b h) -> p b h", h=2),
                 in_=x_turned[token][:].rearrange("p h b -> p b h"),
@@ -148,7 +148,7 @@ def tile_npertokenswishglu_basis_pa_kernel(
             if uses_gram(slot, unit):
                 for block in range(BLOCKS):
                     for j in range(PACK):
-                        w_block = slot_weights[slot][:, unit, j, block * P : (block + 1) * P]
+                        w_block = slot_weights[slot][:, j, unit, block * P : (block + 1) * P]
                         nc.tensor.matmul(
                             out=w_T[:, block * P : (block + 1) * P],
                             lhsT=w_block,
@@ -160,7 +160,7 @@ def tile_npertokenswishglu_basis_pa_kernel(
                 words = slot_weights[slot][:].bitcast(F32)
                 for j in range(PACK):
                     nc.tensor.transpose(
-                        w_T[:, j * P : (j + 1) * P], words[:, unit, j, :], ident_f32[:]
+                        w_T[:, j * P : (j + 1) * P], words[:, j, unit, :], ident_f32[:]
                     )
             weights_T[slot, unit] = w_T
 
@@ -199,12 +199,10 @@ def tile_npertokenswishglu_basis_pa_kernel(
                 )
 
         def invert_norms(slot):
-            clamped = small.tile([P, UNITS * BLOCKS], F32, name="clamped", tag="clamped")
-            nc.gpsimd.tensor_scalar(
-                out=clamped[:], in0=square_sums[slot][:], scalar1=EPS * EPS, scalar2=None, op0=ALU.max
-            )
             inverse = small.tile([P, UNITS * BLOCKS], F32, name="inverse", tag="inverse")
-            nc.gpsimd.tensor_tensor(out=inverse[:], in0=clamped[:], in1=minus_half[:], op=ALU.pow)
+            nc.gpsimd.tensor_tensor(
+                out=inverse[:], in0=square_sums[slot][:], in1=minus_half[:], op=ALU.pow
+            )
             inverse_norms[slot] = inverse
 
         def spread_inverse_norms(slot):
@@ -223,35 +221,35 @@ def tile_npertokenswishglu_basis_pa_kernel(
             spread_norms[slot] = spread
 
         def copy_inverse(slot):
-            rows = small.tile([P, UNITS, G_FEATURES], F32, name="inverse_rows", tag="inverse_rows")
-            nc.scalar.copy(
+            rows = small.tile([P, G_COLUMNS], F32, name="inverse_rows", tag="inverse_rows")
+            nc.vector.tensor_scalar(
                 out=rows[:],
-                in_=spread_norms[slot][:].rearrange("p (u f) -> p u f", u=UNITS)[:, :, V_FEATURES:],
+                in0=spread_norms[slot][:, V_COLUMNS:],
+                scalar1=1.0 / EPS,
+                scalar2=None,
+                op0=ALU.min,
             )
             inverse_rows[slot] = rows
 
         def normalise(slot):
             grouped = work.tile(
-                [P, UNITS * F_SLOT * PACK], BF16, name="grouped", tag="grouped", bufs=1, align_bytes=64
+                [P, UNITS * F_SLOT, PACK], BF16, name="grouped", tag="grouped", bufs=1, align_bytes=64
             )
-            nc.vector.tensor_tensor(
-                out=grouped[:].rearrange("p (u f j) -> p u f j", u=UNITS, j=PACK)[:, :, :V_FEATURES, :],
-                in0=slot_weights[slot][:].rearrange("p u j f -> p u f j")[:, :, :V_FEATURES, :],
-                in1=spread_norms[slot][:]
-                .rearrange("p (u f) -> p u f", u=UNITS)[:, :, :V_FEATURES]
-                .unsqueeze(3)
-                .to_broadcast([P, UNITS, V_FEATURES, PACK]),
-                op=ALU.mult,
+            nc.vector.scalar_tensor_tensor(
+                out=grouped[:, :V_COLUMNS, :],
+                in0=spread_norms[slot][:, :V_COLUMNS].unsqueeze(2).to_broadcast([P, V_COLUMNS, PACK]),
+                scalar=1.0 / EPS,
+                in1=slot_weights[slot][:].rearrange("p j u f -> p (u f) j")[:, :V_COLUMNS, :],
+                op0=ALU.min,
+                op1=ALU.mult,
             )
             normalised[slot] = grouped
 
         def normalise_rest(slot):
             nc.gpsimd.tensor_tensor(
-                out=normalised[slot][:].rearrange("p (u f j) -> p u f j", u=UNITS, j=PACK)[
-                    :, :, V_FEATURES:, :
-                ],
-                in0=slot_weights[slot][:].rearrange("p u j f -> p u f j")[:, :, V_FEATURES:, :],
-                in1=inverse_rows[slot][:].unsqueeze(3).to_broadcast([P, UNITS, G_FEATURES, PACK]),
+                out=normalised[slot][:, V_COLUMNS:, :],
+                in0=slot_weights[slot][:].rearrange("p j u f -> p (u f) j")[:, V_COLUMNS:, :],
+                in1=inverse_rows[slot][:].unsqueeze(2).to_broadcast([P, G_COLUMNS, PACK]),
                 op=ALU.mult,
             )
 
@@ -263,7 +261,9 @@ def tile_npertokenswishglu_basis_pa_kernel(
                 [P, UNITS * F_SLOT], U8, name="w_scales", tag="w_scales", align_bytes=64
             )
             nc.vector.quantize_mx(
-                out=codes[slot][:].bitcast(FP8X4), scales=scales[slot][:], in_=normalised[slot][:]
+                out=codes[slot][:].bitcast(FP8X4),
+                scales=scales[slot][:],
+                in_=normalised[slot][:].rearrange("p c j -> p (c j)"),
             )
 
         def multiply(slot):
@@ -354,12 +354,12 @@ def tile_npertokenswishglu_basis_pa_kernel(
             else:
                 run(sum_squares, t + 3, GATE)
             run(transpose_weights, t + 4, UP)
+            run(copy_inverse, t)
             run(normalise, t)
             run(normalise_rest, t)
             run(invert_norms, t + 2)
             run(apply_silu, t - 1)
             run(sum_squares, t + 3, UP)
-            run(copy_inverse, t + 1)
             if t in turn_at:
                 transpose_x(turn_at[t])
             if t == -4:

@@ -220,37 +220,55 @@ def tile_npertokenswishglu_basis_pa_kernel(
                     )
             spread_norms[slot] = spread
 
+        def gpsimd_columns(slot):
+            stop = F_SLOT if slot == SLOTS - 1 else UNITS * F_SLOT
+            return slice(stop - G_COLUMNS, stop)
+
         def copy_inverse(slot):
             rows = small.tile([P, G_COLUMNS], F32, name="inverse_rows", tag="inverse_rows")
             nc.vector.tensor_scalar(
                 out=rows[:],
-                in0=spread_norms[slot][:, V_COLUMNS:],
+                in0=spread_norms[slot][:, gpsimd_columns(slot)],
                 scalar1=1.0 / EPS,
                 scalar2=None,
                 op0=ALU.min,
             )
             inverse_rows[slot] = rows
 
+        def normalise_columns(slot, columns):
+            width = columns.stop - columns.start
+            nc.vector.scalar_tensor_tensor(
+                out=normalised[slot][:, columns, :],
+                in0=spread_norms[slot][:, columns].unsqueeze(2).to_broadcast([P, width, PACK]),
+                scalar=1.0 / EPS,
+                in1=slot_weights[slot][:].rearrange("p j u f -> p (u f) j")[:, columns, :],
+                op0=ALU.min,
+                op1=ALU.mult,
+            )
+
         def normalise(slot):
             grouped = work.tile(
                 [P, UNITS * F_SLOT, PACK], BF16, name="grouped", tag="grouped", bufs=1, align_bytes=64
             )
-            nc.vector.scalar_tensor_tensor(
-                out=grouped[:, :V_COLUMNS, :],
-                in0=spread_norms[slot][:, :V_COLUMNS].unsqueeze(2).to_broadcast([P, V_COLUMNS, PACK]),
-                scalar=1.0 / EPS,
-                in1=slot_weights[slot][:].rearrange("p j u f -> p (u f) j")[:, :V_COLUMNS, :],
-                op0=ALU.min,
-                op1=ALU.mult,
-            )
             normalised[slot] = grouped
+            if slot == SLOTS - 1:
+                normalise_columns(slot, slice(F_SLOT, UNITS * F_SLOT))
+            else:
+                normalise_columns(slot, slice(0, V_COLUMNS))
 
         def normalise_rest(slot):
             nc.gpsimd.tensor_tensor(
-                out=normalised[slot][:, V_COLUMNS:, :],
-                in0=slot_weights[slot][:].rearrange("p j u f -> p (u f) j")[:, V_COLUMNS:, :],
+                out=normalised[slot][:, gpsimd_columns(slot), :],
+                in0=slot_weights[slot][:].rearrange("p j u f -> p (u f) j")[:, gpsimd_columns(slot), :],
                 in1=inverse_rows[slot][:].unsqueeze(2).to_broadcast([P, G_COLUMNS, PACK]),
                 op=ALU.mult,
+            )
+
+        def quantise_columns(slot, columns):
+            nc.vector.quantize_mx(
+                out=codes[slot][:, columns].bitcast(FP8X4),
+                scales=scales[slot][:, columns],
+                in_=normalised[slot][:, columns, :].rearrange("p c j -> p (c j)"),
             )
 
         def quantise(slot):
@@ -260,28 +278,35 @@ def tile_npertokenswishglu_basis_pa_kernel(
             scales[slot] = work.tile(
                 [P, UNITS * F_SLOT], U8, name="w_scales", tag="w_scales", align_bytes=64
             )
-            nc.vector.quantize_mx(
-                out=codes[slot][:].bitcast(FP8X4),
-                scales=scales[slot][:],
-                in_=normalised[slot][:].rearrange("p c j -> p (c j)"),
-            )
+            if slot == SLOTS - 1:
+                quantise_columns(slot, slice(F_SLOT, UNITS * F_SLOT))
+                multiply_unit(slot, UP)
+                normalise_columns(slot, slice(0, F_SLOT - G_COLUMNS))
+                quantise_columns(slot, slice(0, F_SLOT))
+                multiply_unit(slot, GATE)
+            else:
+                quantise_columns(slot, slice(0, UNITS * F_SLOT))
+
+        def multiply_unit(slot, unit):
+            token = place(slot)[0]
+            product = psum.tile([P, BLOCKS, B], F32, name="product", tag="product%d" % unit)
+            for block in range(BLOCKS):
+                w_cols = slice((unit * BLOCKS + block) * P, (unit * BLOCKS + block + 1) * P)
+                nc.tensor.matmul_mx(
+                    out=product[:, block, :],
+                    lhsT=codes[slot][:, w_cols].bitcast(FP8X4),
+                    lhsT_scale=scales[slot][:, w_cols],
+                    rhs=x_codes[token][:].bitcast(FP8X4),
+                    rhs_scale=x_scales[token][:],
+                    start=True,
+                    stop=True,
+                )
+            products[slot, unit] = product
 
         def multiply(slot):
-            token = place(slot)[0]
-            for unit in range(UNITS):
-                product = psum.tile([P, BLOCKS, B], F32, name="product", tag="product%d" % unit)
-                for block in range(BLOCKS):
-                    w_cols = slice((unit * BLOCKS + block) * P, (unit * BLOCKS + block + 1) * P)
-                    nc.tensor.matmul_mx(
-                        out=product[:, block, :],
-                        lhsT=codes[slot][:, w_cols].bitcast(FP8X4),
-                        lhsT_scale=scales[slot][:, w_cols],
-                        rhs=x_codes[token][:].bitcast(FP8X4),
-                        rhs_scale=x_scales[token][:],
-                        start=True,
-                        stop=True,
-                    )
-                products[slot, unit] = product
+            if slot < SLOTS - 1:
+                for unit in range(UNITS):
+                    multiply_unit(slot, unit)
 
         def gain_column(slot, unit, block):
             column = unit * F_BLOCKS + (slot % SLOTS_PER_TOKEN) * BLOCKS + block
@@ -310,24 +335,39 @@ def tile_npertokenswishglu_basis_pa_kernel(
                 )
 
         def transpose_result(slot):
-            result_T = psum.tile([P, HALVES, F_SLOT], F32, name="result_T", tag="result_T")
+            if slot < SLOTS - 1:
+                result_T = psum.tile([P, HALVES, F_SLOT], F32, name="result_T", tag="result_T")
+                halves = [result_T[:, half, :] for half in range(HALVES)]
+                results_T[slot] = result_T
+            else:
+                first = psum.tile([P, F_SLOT], F32, name="first_half", tag="result_T")
+                second = psum.tile([P, F_SLOT], F32, name="second_half", tag="w_T", bufs=3)
+                halves = [first[:], second[:]]
+                results_T[slot] = halves
             for half in range(HALVES):
                 for block in range(BLOCKS):
                     nc.tensor.transpose(
-                        result_T[:, half, block * P : (block + 1) * P],
+                        halves[half][:, block * P : (block + 1) * P],
                         results[slot][:, block, half * P : (half + 1) * P],
                         ident_f32[:],
                     )
-            results_T[slot] = result_T
 
         def store_result(slot):
             token, f0 = place(slot)
             out_sb = work.tile([P, HALVES, F_SLOT], F32, name="out_sb", tag="out_sb", bufs=4)
-            nc.scalar.copy(out=out_sb[:], in_=results_T[slot][:])
-            nc.sync.dma_start(
-                out=out[:, token, f0 : f0 + F_SLOT].rearrange("(h p) f -> p h f", p=P),
-                in_=out_sb[:],
-            )
+            if slot < SLOTS - 1:
+                nc.scalar.copy(out=out_sb[:], in_=results_T[slot][:])
+                nc.sync.dma_start(
+                    out=out[:, token, f0 : f0 + F_SLOT].rearrange("(h p) f -> p h f", p=P),
+                    in_=out_sb[:],
+                )
+            else:
+                for half, copy in enumerate((nc.scalar.copy, nc.vector.tensor_copy)):
+                    copy(out=out_sb[:, half, :], in_=results_T[slot][half])
+                    nc.sync.dma_start(
+                        out=out[half * P : (half + 1) * P, token, f0 : f0 + F_SLOT],
+                        in_=out_sb[:, half, :],
+                    )
 
         def run(stage, slot, *args):
             if 0 <= slot < SLOTS:

@@ -322,17 +322,17 @@ def tile_npertokenswishglu_basis_pa_kernel(
                     scale=gain_column(slot, UP, block),
                 )
 
-        def combine(slot):
-            results[slot] = work.tile([P, BLOCKS, B], F32, name="result", tag="result")
-            for block in range(BLOCKS):
-                nc.vector.scalar_tensor_tensor(
-                    out=results[slot][:, block, :],
-                    in0=products[slot, GATE][:, block, :],
-                    scalar=gain_column(slot, GATE, block),
-                    in1=silu_v[slot][:, block, :],
-                    op0=ALU.mult,
-                    op1=ALU.mult,
-                )
+        def combine(slot, block):
+            if block == 0:
+                results[slot] = work.tile([P, BLOCKS, B], F32, name="result", tag="result")
+            nc.vector.scalar_tensor_tensor(
+                out=results[slot][:, block, :],
+                in0=products[slot, GATE][:, block, :],
+                scalar=gain_column(slot, GATE, block),
+                in1=silu_v[slot][:, block, :],
+                op0=ALU.mult,
+                op1=ALU.mult,
+            )
 
         def transpose_result(slot):
             if slot < SLOTS - 1:
@@ -394,7 +394,6 @@ def tile_npertokenswishglu_basis_pa_kernel(
             else:
                 run(sum_squares, t + 3, GATE)
             run(transpose_weights, t + 4, UP)
-            run(copy_inverse, t)
             run(normalise, t)
             run(normalise_rest, t)
             run(invert_norms, t + 2)
@@ -406,8 +405,10 @@ def tile_npertokenswishglu_basis_pa_kernel(
                 transpose_gains()
             if t == -2:
                 scale_gains()
-            run(combine, t - 1)
+            run(combine, t - 1, 0)
+            run(copy_inverse, t + 1)
             run(quantise, t)
+            run(combine, t - 1, 1)
             if t in turn_at:
                 group_x(turn_at[t])
             if t in quantise_at:

@@ -29,7 +29,7 @@ F_BLOCKS = F // P
 W_AHEAD = 8
 G_COLUMNS = 112
 V_COLUMNS = UNITS * F_SLOT - G_COLUMNS
-GRAM_SLOTS = (0, 3, 6)
+GRAM_SLOTS = [0, 1] + [slot for slot in range(2, SLOTS - 2) if slot % 8 in (0, 3, 6)]
 
 
 def tile_npertokenswishglu_basis_pa_kernel(
@@ -165,7 +165,7 @@ def tile_npertokenswishglu_basis_pa_kernel(
             weights_T[slot, unit] = w_T
 
         def uses_gram(slot, unit):
-            return unit == GATE and slot % 8 in GRAM_SLOTS
+            return unit == GATE and slot in GRAM_SLOTS
 
         def take_diagonal(slot, unit):
             for block in range(BLOCKS):

import math
from contextlib import ExitStack

import concourse.mybir as mybir
from concourse.masks import make_identity

F32 = mybir.dt.float32
BF16 = mybir.dt.bfloat16
U32 = mybir.dt.uint32
U8 = mybir.dt.uint8
FP8X4 = mybir.dt.float8_e4m3fn_x4
ACT = mybir.ActivationFunctionType
ALU = mybir.AluOpType

B, L, D, F = 256, 8, 512, 1024
EPS = 1e-12
FLOPS = 2 * 2 * B * L * D * F

P = 128
PACK = 4
HALVES = B // P
UNITS = 2
GATE, UP = 0, 1
BLOCKS = 2
F_SLOT = BLOCKS * P
SLOTS_PER_TOKEN = F // F_SLOT
SLOTS = L * SLOTS_PER_TOKEN
F_BLOCKS = F // P
W_AHEAD = 8
G_COLUMNS = 112
V_COLUMNS = UNITS * F_SLOT - G_COLUMNS
GRAM_SLOTS = [0, 1] + [slot for slot in range(2, SLOTS - 2) if slot % 8 in (0, 3, 6)]


def tile_npertokenswishglu_basis_pa_kernel(
    tc, x, w_gate_mix, w_up_mix, u_scale_param, v_scale_param, out
):
    nc = tc.nc
    with ExitStack() as ctx:
        const = ctx.enter_context(tc.tile_pool(name="const", bufs=1))
        weights = ctx.enter_context(tc.tile_pool(name="weights", bufs=W_AHEAD + 6))
        work = ctx.enter_context(tc.tile_pool(name="work", bufs=3))
        small = ctx.enter_context(tc.tile_pool(name="small", bufs=6))
        psum = ctx.enter_context(tc.psum_pool(name="psum", bufs=1))

        def place(slot):
            return slot // SLOTS_PER_TOKEN, (slot % SLOTS_PER_TOKEN) * F_SLOT

        slot_weights, x_rows = {}, {}

        def load_weights(slot):
            token, f0 = place(slot)
            w_sb = weights.tile([P, PACK, UNITS, F_SLOT], BF16, name="w_sb", tag="w_sb")
            for unit, w_dram in enumerate((w_gate_mix, w_up_mix)):
                nc.sync.dma_start(
                    out=w_sb[:, :, unit, :],
                    in_=w_dram[token, :, f0 : f0 + F_SLOT].rearrange("(p j) f -> p j f", j=PACK),
                )
            slot_weights[slot] = w_sb

        def load_x(token):
            x_sb = work.tile([P, HALVES, D], BF16, name="x_sb", tag="x_sb", bufs=3)
            nc.sync.dma_start(out=x_sb[:], in_=x[:, token, :].rearrange("(h p) d -> p h d", p=P))
            x_rows[token] = x_sb

        gain_rows = const.tile([P, P], BF16, name="gain_rows")
        nc.vector.memset(gain_rows[:], 0.0)

        load_weights(0)
        load_x(0)
        for unit, gain_dram in enumerate((u_scale_param, v_scale_param)):
            nc.sync.dma_start(
                out=gain_rows[unit * F_BLOCKS : (unit + 1) * F_BLOCKS, :],
                in_=gain_dram.rearrange("o (r c) -> (o r) c", c=P),
            )
        for slot in range(1, W_AHEAD):
            load_weights(slot)
            if slot == SLOTS_PER_TOKEN:
                load_x(1)

        zero = const.tile([P, 1], F32, name="zero")
        nc.vector.memset(zero[:], 0.0)
        table_warm = const.tile([P, 1], F32, name="table_warm")
        nc.scalar.activation(out=table_warm[:], in_=zero[:], func=ACT.Silu)

        ident_f32 = const.tile([P, P], F32, name="ident_f32")
        make_identity(nc, ident_f32[:])
        ident_bf = const.tile([P, P], BF16, name="ident_bf")
        make_identity(nc, ident_bf[:])
        minus_half = const.tile([P, UNITS * BLOCKS], F32, name="minus_half")
        nc.gpsimd.memset(minus_half[:], -0.5)
        gains = const.tile([P, UNITS * F_BLOCKS], F32, name="gains")

        gain_T = psum.tile([P, P], BF16, name="gain_T", tag="result_T")

        def transpose_gains():
            nc.tensor.transpose(gain_T[:], gain_rows[:], ident_bf[:])

        def scale_gains():
            nc.scalar.activation(out=gains[:, :F_BLOCKS], in_=gain_T[:, :F_BLOCKS], func=ACT.Abs)
            nc.scalar.activation(
                out=gains[:, F_BLOCKS:],
                in_=gain_T[:, F_BLOCKS : UNITS * F_BLOCKS],
                func=ACT.Abs,
                scale=math.sqrt(D),
            )

        x_turned, x_grouped, x_codes, x_scales = {}, {}, {}, {}

        def transpose_x(token):
            if token == 0:
                x_T = psum.tile([P, 2, B], F32, name="x_T", tag="product0")
            else:
                x_T = psum.tile([P, 2, B], F32, name="x_T", tag="w_T", bufs=3)
            x_words = x_rows[token][:].bitcast(F32)
            for half in range(HALVES):
                words = x_words[:, half, :].rearrange("p (q h) -> p h q", h=2)
                for h in range(2):
                    nc.tensor.transpose(
                        x_T[:, h, half * P : (half + 1) * P], words[:, h, :], ident_f32[:]
                    )
            x_turned[token] = x_T

        def group_x(token):
            grouped = work.tile([P, B * PACK], BF16, name="x_grouped", tag="x_grouped", align_bytes=64)
            copy = nc.vector.tensor_copy if token == 0 else nc.scalar.copy
            copy(
                out=grouped[:].bitcast(F32).rearrange("p (b h) -> p b h", h=2),
                in_=x_turned[token][:].rearrange("p h b -> p b h"),
            )
            x_grouped[token] = grouped

        def quantise_x(token):
            x_codes[token] = const.tile([P, B], U32, name="x_codes%d" % token, align_bytes=64)
            x_scales[token] = const.tile([P, B], U8, name="x_scales%d" % token, align_bytes=64)
            nc.vector.quantize_mx(
                out=x_codes[token][:].bitcast(FP8X4),
                scales=x_scales[token][:],
                in_=x_grouped[token][:],
            )

        weights_T, square_sums, inverse_norms, spread_norms = {}, {}, {}, {}
        inverse_rows, normalised, codes, scales = {}, {}, {}, {}
        products, silu_v, results, results_T = {}, {}, {}, {}

        def transpose_weights(slot, unit):
            w_T = psum.tile([P, PACK * P], F32, name="w_T", tag="w_T", bufs=3)
            if uses_gram(slot, unit):
                for block in range(BLOCKS):
                    for j in range(PACK):
                        w_block = slot_weights[slot][:, j, unit, block * P : (block + 1) * P]
                        nc.tensor.matmul(
                            out=w_T[:, block * P : (block + 1) * P],
                            lhsT=w_block,
                            rhs=w_block,
                            start=(j == 0),
                            stop=(j == PACK - 1),
                        )
            else:
                words = slot_weights[slot][:].bitcast(F32)
                for j in range(PACK):
                    nc.tensor.transpose(
                        w_T[:, j * P : (j + 1) * P], words[:, j, unit, :], ident_f32[:]
                    )
            weights_T[slot, unit] = w_T

        def uses_gram(slot, unit):
            return unit == GATE and slot in GRAM_SLOTS

        def take_diagonal(slot, unit):
            for block in range(BLOCKS):
                column = unit * BLOCKS + block
                masked = work.tile([P, P], F32, name="masked", tag="masked")
                nc.vector.scalar_tensor_tensor(
                    out=masked[:],
                    in0=weights_T[slot, unit][:, block * P : (block + 1) * P],
                    scalar=1.0,
                    in1=ident_f32[:],
                    op0=ALU.mult,
                    op1=ALU.mult,
                    accum_out=square_sums[slot][:, column : column + 1],
                )

        def new_sums(slot):
            square_sums[slot] = small.tile(
                [P, UNITS * BLOCKS], F32, name="square_sum", tag="square_sum"
            )

        def sum_squares(slot, unit):
            halves_of_words = weights_T[slot, unit][:].bitcast(BF16).rearrange("p (w e) -> p e w", e=2)
            for e in range(2):
                column = unit * BLOCKS + e
                squares = work.tile([P, D], BF16, name="squares", tag="squares", bufs=4)
                nc.scalar.activation(
                    out=squares[:],
                    in_=halves_of_words[:, e, :],
                    func=ACT.Square,
                    accum_out=square_sums[slot][:, column : column + 1],
                )

        def invert_norms(slot):
            inverse = small.tile([P, UNITS * BLOCKS], F32, name="inverse", tag="inverse")
            nc.gpsimd.tensor_tensor(
                out=inverse[:], in0=square_sums[slot][:], in1=minus_half[:], op=ALU.pow
            )
            inverse_norms[slot] = inverse

        def spread_inverse_norms(slot):
            spread = psum.tile([P, UNITS * F_SLOT], F32, name="spread", tag="spread", bufs=2)
            by_column = spread[:].rearrange("p (u q e) -> p u e q", u=UNITS, e=2)
            for unit in range(UNITS):
                for e in range(2):
                    column = unit * BLOCKS + e
                    nc.tensor.transpose(
                        spread[:, column * P : (column + 1) * P]
                        if uses_gram(slot, unit)
                        else by_column[:, unit, e, :],
                        inverse_norms[slot][:, column : column + 1].to_broadcast([P, P]),
                        ident_f32[:],
                    )
            spread_norms[slot] = spread

        def gpsimd_columns(slot):
            stop = F_SLOT if slot == SLOTS - 1 else UNITS * F_SLOT
            return slice(stop - G_COLUMNS, stop)

        def copy_inverse(slot):
            rows = small.tile([P, G_COLUMNS], F32, name="inverse_rows", tag="inverse_rows")
            nc.vector.tensor_scalar(
                out=rows[:],
                in0=spread_norms[slot][:, gpsimd_columns(slot)],
                scalar1=1.0 / EPS,
                scalar2=None,
                op0=ALU.min,
            )
            inverse_rows[slot] = rows

        def normalise_columns(slot, columns):
            width = columns.stop - columns.start
            nc.vector.scalar_tensor_tensor(
                out=normalised[slot][:, columns, :],
                in0=spread_norms[slot][:, columns].unsqueeze(2).to_broadcast([P, width, PACK]),
                scalar=1.0 / EPS,
                in1=slot_weights[slot][:].rearrange("p j u f -> p (u f) j")[:, columns, :],
                op0=ALU.min,
                op1=ALU.mult,
            )

        def normalise(slot):
            grouped = work.tile(
                [P, UNITS * F_SLOT, PACK], BF16, name="grouped", tag="grouped", bufs=1, align_bytes=64
            )
            normalised[slot] = grouped
            if slot == SLOTS - 1:
                normalise_columns(slot, slice(F_SLOT, UNITS * F_SLOT))
            else:
                normalise_columns(slot, slice(0, V_COLUMNS))

        def normalise_rest(slot):
            nc.gpsimd.tensor_tensor(
                out=normalised[slot][:, gpsimd_columns(slot), :],
                in0=slot_weights[slot][:].rearrange("p j u f -> p (u f) j")[:, gpsimd_columns(slot), :],
                in1=inverse_rows[slot][:].unsqueeze(2).to_broadcast([P, G_COLUMNS, PACK]),
                op=ALU.mult,
            )

        def quantise_columns(slot, columns):
            nc.vector.quantize_mx(
                out=codes[slot][:, columns].bitcast(FP8X4),
                scales=scales[slot][:, columns],
                in_=normalised[slot][:, columns, :].rearrange("p c j -> p (c j)"),
            )

        def quantise(slot):
            codes[slot] = work.tile(
                [P, UNITS * F_SLOT], U32, name="w_codes", tag="w_codes", align_bytes=64
            )
            scales[slot] = work.tile(
                [P, UNITS * F_SLOT], U8, name="w_scales", tag="w_scales", align_bytes=64
            )
            if slot == SLOTS - 1:
                quantise_columns(slot, slice(F_SLOT, UNITS * F_SLOT))
                multiply_unit(slot, UP)
                normalise_columns(slot, slice(0, F_SLOT - G_COLUMNS))
                quantise_columns(slot, slice(0, F_SLOT))
                multiply_unit(slot, GATE)
            else:
                quantise_columns(slot, slice(0, UNITS * F_SLOT))

        def multiply_unit(slot, unit):
            token = place(slot)[0]
            product = psum.tile([P, BLOCKS, B], F32, name="product", tag="product%d" % unit)
            for block in range(BLOCKS):
                w_cols = slice((unit * BLOCKS + block) * P, (unit * BLOCKS + block + 1) * P)
                nc.tensor.matmul_mx(
                    out=product[:, block, :],
                    lhsT=codes[slot][:, w_cols].bitcast(FP8X4),
                    lhsT_scale=scales[slot][:, w_cols],
                    rhs=x_codes[token][:].bitcast(FP8X4),
                    rhs_scale=x_scales[token][:],
                    start=True,
                    stop=True,
                )
            products[slot, unit] = product

        def multiply(slot):
            if slot < SLOTS - 1:
                for unit in range(UNITS):
                    multiply_unit(slot, unit)

        def gain_column(slot, unit, block):
            column = unit * F_BLOCKS + (slot % SLOTS_PER_TOKEN) * BLOCKS + block
            return gains[:, column : column + 1]

        def apply_silu(slot):
            silu_v[slot] = work.tile([P, BLOCKS, B], F32, name="silu_v", tag="silu_v")
            for block in range(BLOCKS):
                nc.scalar.activation(
                    out=silu_v[slot][:, block, :],
                    in_=products[slot, UP][:, block, :],
                    func=ACT.Silu,
                    scale=gain_column(slot, UP, block),
                )

        def combine(slot, block):
            if block == 0:
                results[slot] = work.tile([P, BLOCKS, B], F32, name="result", tag="result")
            nc.vector.scalar_tensor_tensor(
                out=results[slot][:, block, :],
                in0=products[slot, GATE][:, block, :],
                scalar=gain_column(slot, GATE, block),
                in1=silu_v[slot][:, block, :],
                op0=ALU.mult,
                op1=ALU.mult,
            )

        def transpose_result(slot):
            if slot < SLOTS - 1:
                result_T = psum.tile([P, HALVES, F_SLOT], F32, name="result_T", tag="result_T")
                halves = [result_T[:, half, :] for half in range(HALVES)]
                results_T[slot] = result_T
            else:
                first = psum.tile([P, F_SLOT], F32, name="first_half", tag="result_T")
                second = psum.tile([P, F_SLOT], F32, name="second_half", tag="w_T", bufs=3)
                halves = [first[:], second[:]]
                results_T[slot] = halves
            for half in range(HALVES):
                for block in range(BLOCKS):
                    nc.tensor.transpose(
                        halves[half][:, block * P : (block + 1) * P],
                        results[slot][:, block, half * P : (half + 1) * P],
                        ident_f32[:],
                    )

        def store_result(slot):
            token, f0 = place(slot)
            out_sb = work.tile([P, HALVES, F_SLOT], F32, name="out_sb", tag="out_sb", bufs=4)
            if slot < SLOTS - 1:
                nc.scalar.copy(out=out_sb[:], in_=results_T[slot][:])
                nc.sync.dma_start(
                    out=out[:, token, f0 : f0 + F_SLOT].rearrange("(h p) f -> p h f", p=P),
                    in_=out_sb[:],
                )
            else:
                for half, copy in enumerate((nc.scalar.copy, nc.vector.tensor_copy)):
                    copy(out=out_sb[:, half, :], in_=results_T[slot][half])
                    nc.sync.dma_start(
                        out=out[half * P : (half + 1) * P, token, f0 : f0 + F_SLOT],
                        in_=out_sb[:, half, :],
                    )

        def run(stage, slot, *args):
            if 0 <= slot < SLOTS:
                stage(slot, *args)

        X_LEAD = 5
        turn_at, quantise_at = {-4: 0}, {-3: 0}
        for token in range(1, L):
            turn_at[SLOTS_PER_TOKEN * token - X_LEAD] = token
            quantise_at[SLOTS_PER_TOKEN * token - X_LEAD + 1] = token

        for t in range(-4, SLOTS + 2):
            if t >= -3:
                run(load_weights, t + 3 + W_AHEAD)
            if turn_at.get(t, 0) > 0 and turn_at[t] + 1 < L:
                load_x(turn_at[t] + 1)
            run(multiply, t - 1)
            run(transpose_result, t - 2)
            run(spread_inverse_norms, t + 1)
            run(transpose_weights, t + 4, GATE)
            run(new_sums, t + 3)
            if uses_gram(t + 3, GATE):
                run(take_diagonal, t + 3, GATE)
            else:
                run(sum_squares, t + 3, GATE)
            run(transpose_weights, t + 4, UP)
            run(normalise, t)
            run(normalise_rest, t)
            run(invert_norms, t + 2)
            run(apply_silu, t - 1)
            run(sum_squares, t + 3, UP)
            if t in turn_at:
                transpose_x(turn_at[t])
            if t == -4:
                transpose_gains()
            if t == -2:
                scale_gains()
            run(combine, t - 1, 0)
            run(copy_inverse, t + 1)
            run(quantise, t)
            run(combine, t - 1, 1)
            if t in turn_at:
                group_x(turn_at[t])
            if t in quantise_at:
                quantise_x(quantise_at[t])
            run(store_result, t - 2)
